import numpy as np
import ml_dtypes


def mxq(x, axis, fmt="e4m3"):
    dtype, down = {"e4m3": (ml_dtypes.float8_e4m3fn, 7), "e5m2": (ml_dtypes.float8_e5m2, 14)}[fmt]
    v = np.moveaxis(np.asarray(x, np.float32).astype(ml_dtypes.bfloat16).astype(np.float64), axis, -1)
    blocks = v.reshape(v.shape[:-1] + (-1, 32))
    amax = np.abs(blocks).max(-1, keepdims=True)
    byte = np.maximum(np.where(amax > 0, np.frexp(amax)[1] - 1 + 127, 0) - down, 1)
    scale = np.exp2(byte - 127.0)
    codes = (blocks / scale).astype(np.float32).astype(dtype).astype(np.float64)
    return np.moveaxis((codes * scale).reshape(v.shape), -1, axis)


WIDE = False


def mx_kscale(k):
    if not WIDE:
        return np.ones(k)
    levels = np.array([10, -10, 5, -5, 0])
    if k % 512:
        return np.exp2(np.random.permutation(np.resize(levels, k // 32))).repeat(32)
    a = np.empty((k // 512, 16))
    for p in range(k // 512):
        a[p, :8] = np.random.permutation(np.resize(levels, 8))
        for g in range(8):
            far = levels[np.abs(levels - a[p, g]) >= 10]
            a[p, g + 8] = far[np.random.randint(len(far))]
    return np.exp2(a.ravel()).repeat(32)


BF16 = ml_dtypes.bfloat16


def bf(x):
    return np.asarray(x, np.float32).astype(BF16)


def f64(x):
    return np.asarray(x).astype(np.float64)


H, N, S, T, L, K = 2, 2, 256, 2048, 4096, 512
NH = N * H


def rel_shift(p):
    zero_pad = np.zeros((NH, S, 1))
    padded = np.concatenate([zero_pad, p], axis=2)
    padded = padded.reshape(NH, T + 1, S)
    return padded[:, 1:, :].reshape(NH, S, T)


def setup_inputs():
    s = mx_kscale(K)
    return {"queries": bf(np.random.standard_normal((NH, S, K)) * s),
            "v_bias": bf(np.random.standard_normal((1, H, 1, K)) / np.sqrt(K) * s),
            "R": bf(np.random.standard_normal((H, L, K)) / s)}


def reference(queries, v_bias, R):
    q = (f64(queries) * K ** -0.5).reshape(N, H, S, K)
    q_v = q + f64(v_bias)
    r = f64(R)[:, :T, :]
    pos = mxq(q_v, 3, "e4m3") @ mxq(r, 2, "e4m3").transpose(0, 2, 1)
    return rel_shift(pos.reshape(NH, S, T))

@@ -1,0 +1,165 @@
+from contextlib import ExitStack
+
+import concourse.mybir as mybir
+from concourse.masks import make_identity
+
+F32 = mybir.dt.float32
+BF16 = mybir.dt.bfloat16
+U32 = mybir.dt.uint32
+U8 = mybir.dt.uint8
+FP8X4 = mybir.dt.float8_e4m3fn_x4
+MULT = mybir.AluOpType.mult
+ADD = mybir.AluOpType.add
+
+P = 128
+HEADS = 2
+SEQS = 2
+BATCH = SEQS * HEADS
+S = 256
+T = 2048
+K = 512
+PACK = 4
+WORDS = K // 2
+S_BLOCKS = S // P
+T_CHUNK = 512
+T_CHUNKS = T // T_CHUNK
+ROWS = T_CHUNK // P
+PAD = 8
+WIDE = T + 1
+DROP = S
+GROUP = 2
+
+FLOPS = 2 * BATCH * S * T * K
+BYTES = 2 * (BATCH * S * K + HEADS * K + HEADS * T * K) + 4 * BATCH * S * T
+
+
+def tile_relativepositionsdpa_pa_kernel(tc, queries, v_bias, R, out):
+    nc = tc.nc
+    with ExitStack() as ctx:
+        keep = ctx.enter_context(tc.tile_pool(name="keep", bufs=1))
+        stage = ctx.enter_context(tc.tile_pool(name="stage", bufs=3))
+        psum = ctx.enter_context(tc.psum_pool(name="psum", bufs=4))
+
+        ident = keep.tile([P, P], F32)
+        make_identity(nc, ident[:])
+        bias_rows = keep.tile([P, K], BF16)
+        nc.vector.memset(bias_rows[:], 0.0)
+        out_rows = [keep.tile([P, PAD + T], F32, name="out_rows%d" % i) for i in range(BATCH * S_BLOCKS)]
+        for rows in out_rows:
+            nc.vector.memset(rows[:, 0:PAD], 0.0)
+
+        nc.sync.dma_start(out=bias_rows[0:HEADS, :], in_=v_bias.rearrange("o h i k -> (o h i) k"))
+        q_raw = [keep.tile([P, S_BLOCKS * K], BF16, name="q_raw%d" % b) for b in range(BATCH)]
+        r_raw = [keep.tile([P, ROWS * K], BF16, name="r_raw%d" % i) for i in range(HEADS * T_CHUNKS)]
+        for h in range(HEADS):
+            for b in range(h, BATCH, HEADS):
+                nc.sync.dma_start(
+                    out=q_raw[b][:].rearrange("p (j k) -> p j k", j=S_BLOCKS),
+                    in_=queries[b].rearrange("(j p) k -> p j k", p=P),
+                )
+            for c in range(T_CHUNKS):
+                nc.sync.dma_start(
+                    out=r_raw[h * T_CHUNKS + c][:],
+                    in_=R[h, c * T_CHUNK : (c + 1) * T_CHUNK, :].rearrange("(p j) k -> p (j k)", j=ROWS),
+                )
+
+        bias_sb = keep.tile([P, HEADS * PACK], BF16)
+        bias_t = psum.tile([P, 2 * P], F32, tag="flip")
+        for u in range(2):
+            nc.tensor.transpose(bias_t[:, u * P : (u + 1) * P], bias_rows[:].bitcast(F32)[:, u:WORDS:2], ident[:])
+        nc.vector.tensor_copy(
+            out=bias_sb[:].bitcast(F32).rearrange("p (h u) -> p h u", u=2),
+            in_=bias_t[:].rearrange("p (u s) -> p s u", u=2)[:, 0:HEADS, :],
+        )
+
+        q_codes = keep.tile([P, BATCH, S], U32, align_bytes=64)
+        q_scales = keep.tile([P, BATCH, S], U8, align_bytes=64)
+        r_codes = keep.tile([P, HEADS * T_CHUNKS, T_CHUNK], U32, align_bytes=64)
+        r_scales = keep.tile([P, HEADS * T_CHUNKS, T_CHUNK], U8, align_bytes=64)
+
+        def prepare_queries(b):
+            h = b % HEADS
+            words = q_raw[b][:].bitcast(F32)
+            flip = psum.tile([P, 2 * S], F32, tag="flip")
+            for u in range(2):
+                for j in range(S_BLOCKS):
+                    nc.tensor.transpose(
+                        flip[:, u * S + j * P : u * S + (j + 1) * P],
+                        words[:, j * WORDS + u : (j + 1) * WORDS : 2],
+                        ident[:],
+                    )
+            q_pairs = stage.tile([P, S * PACK], BF16)
+            nc.scalar.copy(
+                out=q_pairs[:].bitcast(F32).rearrange("p (s u) -> p s u", u=2),
+                in_=flip[:].rearrange("p (u s) -> p s u", u=2),
+            )
+            q_v = stage.tile([P, S * PACK], BF16, align_bytes=64)
+            nc.vector.scalar_tensor_tensor(
+                out=q_v[:].rearrange("p (s t) -> p s t", t=PACK),
+                in0=q_pairs[:].rearrange("p (s t) -> p s t", t=PACK),
+                scalar=K**-0.5,
+                in1=bias_sb[:, h * PACK : (h + 1) * PACK].unsqueeze(1).to_broadcast([P, S, PACK]),
+                op0=MULT,
+                op1=ADD,
+            )
+            nc.vector.quantize_mx(out=q_codes[:, b, :].bitcast(FP8X4), scales=q_scales[:, b, :], in_=q_v[:])
+
+        def prepare_table(i):
+            words = r_raw[i][:].bitcast(F32)
+            grouped = stage.tile([P, T_CHUNK * PACK], BF16, align_bytes=64)
+            grouped_words = grouped[:].bitcast(F32).rearrange("p (n g f) -> p n g f", g=2, f=4)
+            for g in range(2):
+                flip = psum.tile([P, 4 * P], F32, tag="flip")
+                for f in range(4):
+                    j, u = 2 * g + f // 2, f % 2
+                    nc.tensor.transpose(
+                        flip[:, f * P : (f + 1) * P],
+                        words[:, j * WORDS + u : (j + 1) * WORDS : 2],
+                        ident[:],
+                    )
+                nc.scalar.copy(out=grouped_words[:, :, g, :], in_=flip[:].rearrange("p (f n) -> p n f", f=4))
+            nc.vector.quantize_mx(out=r_codes[:, i, :].bitcast(FP8X4), scales=r_scales[:, i, :], in_=grouped[:])
+
+        def products(b, j, g):
+            h = b % HEADS
+            rows = out_rows[b * S_BLOCKS + j]
+            for c in range(g * GROUP, (g + 1) * GROUP):
+                i = h * T_CHUNKS + c
+                acc = psum.tile([P, T_CHUNK], F32, tag="acc")
+                nc.tensor.matmul_mx(
+                    out=acc[:],
+                    lhsT=q_codes[:, b, j * P : (j + 1) * P].bitcast(FP8X4),
+                    lhsT_scale=q_scales[:, b, j * P : (j + 1) * P],
+                    rhs=r_codes[:, i, :].bitcast(FP8X4),
+                    rhs_scale=r_scales[:, i, :],
+                    start=True,
+                    stop=True,
+                )
+                dst = rows[:, PAD + c * T_CHUNK : PAD + (c + 1) * T_CHUNK]
+                if c % 2 == 0:
+                    nc.vector.tensor_copy(out=dst, in_=acc[:])
+                else:
+                    nc.scalar.copy(out=dst, in_=acc[:])
+            lo = 1 + g * GROUP * T_CHUNK if g > 0 else 0
+            hi = 1 + (g + 1) * GROUP * T_CHUNK
+            flat = out[b].rearrange("s t -> (s t)")
+            if j == 0:
+                cut = flat[0 : P * WIDE].rearrange("(p w) -> p w", w=WIDE)
+                if lo == 0:
+                    nc.sync.dma_start(out=cut[15 : P - 1, WIDE - DROP : WIDE], in_=rows[16:P, PAD - 1 : PAD - 1 + DROP])
+                    nc.sync.dma_start(out=cut[0:15, WIDE - DROP : WIDE], in_=rows[1:16, PAD - 1 : PAD - 1 + DROP])
+                    lo = DROP
+                nc.sync.dma_start(out=cut[:, lo - DROP : hi - DROP], in_=rows[:, PAD - 1 + lo : PAD - 1 + hi])
+            else:
+                cut = flat[P * WIDE - DROP : S * T].rearrange("(p w) -> p w", w=WIDE)
+                nc.sync.dma_start(out=cut[:, lo:hi], in_=rows[:, PAD - 1 + lo : PAD - 1 + hi])
+
+        for h in range(HEADS):
+            for b in range(h, BATCH, HEADS):
+                prepare_queries(b)
+            for g in range(T_CHUNKS // GROUP):
+                for c in range(g * GROUP, (g + 1) * GROUP):
+                    prepare_table(h * T_CHUNKS + c)
+                for b in range(h, BATCH, HEADS):
+                    for j in range(S_BLOCKS):
+                        products(b, j, g)

@@ -154,12 +154,22 @@ def tile_relativepositionsdpa_pa_kernel(tc, queries, v_bias, R, out):
                 cut = flat[P * WIDE - DROP : S * T].rearrange("(p w) -> p w", w=WIDE)
                 nc.sync.dma_start(out=cut[:, lo:hi], in_=rows[:, PAD - 1 + lo : PAD - 1 + hi])
 
-        for h in range(HEADS):
-            for b in range(h, BATCH, HEADS):
-                prepare_queries(b)
-            for g in range(T_CHUNKS // GROUP):
-                for c in range(g * GROUP, (g + 1) * GROUP):
-                    prepare_table(h * T_CHUNKS + c)
-                for b in range(h, BATCH, HEADS):
-                    for j in range(S_BLOCKS):
-                        products(b, j, g)
+        units = [(h, g, b) for h in range(HEADS) for g in range(T_CHUNKS // GROUP) for b in range(h, BATCH, HEADS)]
+        prepare_queries(0)
+        prepare_queries(2)
+        prepare_table(0)
+        prepare_table(1)
+        ahead = {
+            (0, 0, 0): lambda: prepare_table(2),
+            (0, 0, 2): lambda: (prepare_table(3), prepare_queries(1)),
+            (0, 1, 0): lambda: prepare_table(4),
+            (0, 1, 2): lambda: (prepare_table(5), prepare_queries(3)),
+            (1, 0, 1): lambda: prepare_table(6),
+            (1, 0, 3): lambda: prepare_table(7),
+        }
+        for unit in units:
+            h, g, b = unit
+            for j in range(S_BLOCKS):
+                products(b, j, g)
+            if unit in ahead:
+                ahead[unit]()

@@ -42,6 +42,10 @@ def tile_relativepositionsdpa_pa_kernel(tc, queries, v_bias, R, out):
 
         ident = keep.tile([P, P], F32)
         make_identity(nc, ident[:])
+        zeros = keep.tile([P, P], F32)
+        nc.vector.memset(zeros[:], 0.0)
+        zeros_bf = keep.tile([P, P], BF16)
+        nc.vector.memset(zeros_bf[:], 0.0)
         bias_rows = keep.tile([P, K], BF16)
         nc.vector.memset(bias_rows[:], 0.0)
         out_rows = [keep.tile([P, PAD + T], F32, name="out_rows%d" % i) for i in range(BATCH * S_BLOCKS)]
@@ -62,6 +66,14 @@ def tile_relativepositionsdpa_pa_kernel(tc, queries, v_bias, R, out):
                     out=r_raw[h * T_CHUNKS + c][:],
                     in_=R[h, c * T_CHUNK : (c + 1) * T_CHUNK, :].rearrange("(p j) k -> p (j k)", j=ROWS),
                 )
+
+        warm = psum.tile([P, P], F32, tag="flip")
+        for n in range(8):
+            nc.tensor.matmul(warm[:], lhsT=zeros[:], rhs=zeros[:], start=True, stop=True)
+
+        def keep_warm(loaded):
+            idle = psum.tile([P, T_CHUNK], F32, tag="flip")
+            nc.tensor.matmul(idle[:], lhsT=zeros_bf[:], rhs=loaded[:, 0:T_CHUNK], start=True, stop=True)
 
         bias_sb = keep.tile([P, HEADS * PACK], BF16)
         bias_t = psum.tile([P, 2 * P], F32, tag="flip")
@@ -156,9 +168,17 @@ def tile_relativepositionsdpa_pa_kernel(tc, queries, v_bias, R, out):
 
         units = [(h, g, b) for h in range(HEADS) for g in range(T_CHUNKS // GROUP) for b in range(h, BATCH, HEADS)]
         prepare_queries(0)
+        keep_warm(q_raw[0])
+        keep_warm(q_raw[0])
         prepare_queries(2)
+        keep_warm(q_raw[2])
+        keep_warm(q_raw[2])
         prepare_table(0)
+        keep_warm(r_raw[0])
+        keep_warm(r_raw[0])
         prepare_table(1)
+        keep_warm(r_raw[1])
+        keep_warm(r_raw[1])
         ahead = {
             (0, 0, 0): lambda: prepare_table(2),
             (0, 0, 2): lambda: (prepare_table(3), prepare_queries(1)),

@@ -28,6 +28,7 @@ PAD = 8
 WIDE = T + 1
 DROP = S
 GROUP = 2
+HEAD_ORDER = (1, 0)
 
 FLOPS = 2 * BATCH * S * T * K
 BYTES = 2 * (BATCH * S * K + HEADS * K + HEADS * T * K) + 4 * BATCH * S * T
@@ -55,12 +56,9 @@ def tile_relativepositionsdpa_pa_kernel(tc, queries, v_bias, R, out):
         nc.sync.dma_start(out=bias_rows[0:HEADS, :], in_=v_bias.rearrange("o h i k -> (o h i) k"))
         q_raw = [keep.tile([P, S_BLOCKS * K], BF16, name="q_raw%d" % b) for b in range(BATCH)]
         r_raw = [keep.tile([P, ROWS * K], BF16, name="r_raw%d" % i) for i in range(HEADS * T_CHUNKS)]
-        for h in range(HEADS):
+        for h in HEAD_ORDER:
             for b in range(h, BATCH, HEADS):
-                nc.sync.dma_start(
-                    out=q_raw[b][:].rearrange("p (j k) -> p j k", j=S_BLOCKS),
-                    in_=queries[b].rearrange("(j p) k -> p j k", p=P),
-                )
+                nc.sync.dma_start(out=q_raw[b][:], in_=queries[b].rearrange("(p e) k -> p (e k)", e=2))
             for c in range(T_CHUNKS):
                 nc.sync.dma_start(
                     out=r_raw[h * T_CHUNKS + c][:],
@@ -68,7 +66,7 @@ def tile_relativepositionsdpa_pa_kernel(tc, queries, v_bias, R, out):
                 )
 
         warm = psum.tile([P, P], F32, tag="flip")
-        for n in range(8):
+        for n in range(4):
             nc.tensor.matmul(warm[:], lhsT=zeros[:], rhs=zeros[:], start=True, stop=True)
 
         def keep_warm(loaded):
@@ -92,18 +90,14 @@ def tile_relativepositionsdpa_pa_kernel(tc, queries, v_bias, R, out):
         def prepare_queries(b):
             h = b % HEADS
             words = q_raw[b][:].bitcast(F32)
-            flip = psum.tile([P, 2 * S], F32, tag="flip")
-            for u in range(2):
-                for j in range(S_BLOCKS):
-                    nc.tensor.transpose(
-                        flip[:, u * S + j * P : u * S + (j + 1) * P],
-                        words[:, j * WORDS + u : (j + 1) * WORDS : 2],
-                        ident[:],
-                    )
+            flip = psum.tile([P, 4 * P], F32, tag="flip")
+            for f in range(4):
+                at = (f // 2) * WORDS + f % 2
+                nc.tensor.transpose(flip[:, f * P : (f + 1) * P], words[:, at : at + WORDS - 1 : 2], ident[:])
             q_pairs = stage.tile([P, S * PACK], BF16)
             nc.scalar.copy(
-                out=q_pairs[:].bitcast(F32).rearrange("p (s u) -> p s u", u=2),
-                in_=flip[:].rearrange("p (u s) -> p s u", u=2),
+                out=q_pairs[:].bitcast(F32).rearrange("p (n f) -> p n f", f=4),
+                in_=flip[:].rearrange("p (f n) -> p n f", f=4),
             )
             q_v = stage.tile([P, S * PACK], BF16, align_bytes=64)
             nc.vector.scalar_tensor_tensor(
@@ -132,64 +126,70 @@ def tile_relativepositionsdpa_pa_kernel(tc, queries, v_bias, R, out):
                 nc.scalar.copy(out=grouped_words[:, :, g, :], in_=flip[:].rearrange("p (f n) -> p n f", f=4))
             nc.vector.quantize_mx(out=r_codes[:, i, :].bitcast(FP8X4), scales=r_scales[:, i, :], in_=grouped[:])
 
-        def products(b, j, g):
+        def products(b, g):
             h = b % HEADS
+            for j in range(S_BLOCKS):
+                for c in range(g * GROUP, (g + 1) * GROUP):
+                    i = h * T_CHUNKS + c
+                    acc = psum.tile([P, T_CHUNK], F32, tag="acc")
+                    nc.tensor.matmul_mx(
+                        out=acc[:],
+                        lhsT=q_codes[:, b, j * P : (j + 1) * P].bitcast(FP8X4),
+                        lhsT_scale=q_scales[:, b, j * P : (j + 1) * P],
+                        rhs=r_codes[:, i, :].bitcast(FP8X4),
+                        rhs_scale=r_scales[:, i, :],
+                        start=True,
+                        stop=True,
+                    )
+                    dst = out_rows[b * S_BLOCKS + j][:, PAD + c * T_CHUNK : PAD + (c + 1) * T_CHUNK]
+                    if c % 2 == 0:
+                        nc.vector.tensor_copy(out=dst, in_=acc[:])
+                    else:
+                        nc.scalar.copy(out=dst, in_=acc[:])
+                store(b, j, g)
+
+        flat = out.rearrange("b s t -> (b s t)")
+        held = []
+
+        def store(b, j, g):
+            for late in held:
+                late()
+            held.clear()
             rows = out_rows[b * S_BLOCKS + j]
-            for c in range(g * GROUP, (g + 1) * GROUP):
-                i = h * T_CHUNKS + c
-                acc = psum.tile([P, T_CHUNK], F32, tag="acc")
-                nc.tensor.matmul_mx(
-                    out=acc[:],
-                    lhsT=q_codes[:, b, j * P : (j + 1) * P].bitcast(FP8X4),
-                    lhsT_scale=q_scales[:, b, j * P : (j + 1) * P],
-                    rhs=r_codes[:, i, :].bitcast(FP8X4),
-                    rhs_scale=r_scales[:, i, :],
-                    start=True,
-                    stop=True,
-                )
-                dst = rows[:, PAD + c * T_CHUNK : PAD + (c + 1) * T_CHUNK]
-                if c % 2 == 0:
-                    nc.vector.tensor_copy(out=dst, in_=acc[:])
-                else:
-                    nc.scalar.copy(out=dst, in_=acc[:])
             lo = 1 + g * GROUP * T_CHUNK if g > 0 else 0
             hi = 1 + (g + 1) * GROUP * T_CHUNK
-            flat = out[b].rearrange("s t -> (s t)")
-            if j == 0:
-                cut = flat[0 : P * WIDE].rearrange("(p w) -> p w", w=WIDE)
-                if lo == 0:
-                    nc.sync.dma_start(out=cut[15 : P - 1, WIDE - DROP : WIDE], in_=rows[16:P, PAD - 1 : PAD - 1 + DROP])
-                    nc.sync.dma_start(out=cut[0:15, WIDE - DROP : WIDE], in_=rows[1:16, PAD - 1 : PAD - 1 + DROP])
+            if b % HEADS == 0 and j == 0:
+                start, skip = b * S * T, DROP
+                if g == 0:
+                    later = flat[start + WIDE - DROP : start + P * WIDE - DROP].rearrange("(p w) -> p w", w=WIDE)
+                    front = slice(PAD - 1, PAD - 1 + DROP)
+                    nc.sync.dma_start(out=later[P // 2 - 1 : P - 1, 0:DROP], in_=rows[P // 2 : P, front])
+                    held.append(lambda: nc.sync.dma_start(out=later[0 : P // 2, 0:DROP], in_=rows[1 : P // 2 + 1, front]))
                     lo = DROP
-                nc.sync.dma_start(out=cut[:, lo - DROP : hi - DROP], in_=rows[:, PAD - 1 + lo : PAD - 1 + hi])
             else:
-                cut = flat[P * WIDE - DROP : S * T].rearrange("(p w) -> p w", w=WIDE)
-                nc.sync.dma_start(out=cut[:, lo:hi], in_=rows[:, PAD - 1 + lo : PAD - 1 + hi])
+                start, skip = b * S * T + j * P * WIDE - DROP, 0
+            view = flat[start : start + P * WIDE].rearrange("(p w) -> p w", w=WIDE)
+            nc.sync.dma_start(out=view[:, lo - skip : hi - skip], in_=rows[:, PAD - 1 + lo : PAD - 1 + hi])
 
-        units = [(h, g, b) for h in range(HEADS) for g in range(T_CHUNKS // GROUP) for b in range(h, BATCH, HEADS)]
+        prepare_queries(1)
+        keep_warm(q_raw[1])
+        prepare_queries(3)
+        keep_warm(q_raw[3])
+        prepare_table(4)
+        prepare_table(5)
+        products(1, 0)
+        prepare_table(6)
+        products(3, 0)
+        prepare_table(7)
         prepare_queries(0)
-        keep_warm(q_raw[0])
-        keep_warm(q_raw[0])
-        prepare_queries(2)
-        keep_warm(q_raw[2])
-        keep_warm(q_raw[2])
+        products(1, 1)
         prepare_table(0)
-        keep_warm(r_raw[0])
-        keep_warm(r_raw[0])
+        products(3, 1)
         prepare_table(1)
-        keep_warm(r_raw[1])
-        keep_warm(r_raw[1])
-        ahead = {
-            (0, 0, 0): lambda: prepare_table(2),
-            (0, 0, 2): lambda: (prepare_table(3), prepare_queries(1)),
-            (0, 1, 0): lambda: prepare_table(4),
-            (0, 1, 2): lambda: (prepare_table(5), prepare_queries(3)),
-            (1, 0, 1): lambda: prepare_table(6),
-            (1, 0, 3): lambda: prepare_table(7),
-        }
-        for unit in units:
-            h, g, b = unit
-            for j in range(S_BLOCKS):
-                products(b, j, g)
-            if unit in ahead:
-                ahead[unit]()
+        prepare_queries(2)
+        products(0, 0)
+        prepare_table(2)
+        products(2, 0)
+        prepare_table(3)
+        products(0, 1)
+        products(2, 1)

@@ -43,44 +43,35 @@ def tile_relativepositionsdpa_pa_kernel(tc, queries, v_bias, R, out):
 
         ident = keep.tile([P, P], F32)
         make_identity(nc, ident[:])
-        zeros = keep.tile([P, P], F32)
-        nc.vector.memset(zeros[:], 0.0)
-        zeros_bf = keep.tile([P, P], BF16)
-        nc.vector.memset(zeros_bf[:], 0.0)
         bias_rows = keep.tile([P, K], BF16)
-        nc.vector.memset(bias_rows[:], 0.0)
+        nc.vector.memset(bias_rows[:].bitcast(F32), 0.0)
         out_rows = [keep.tile([P, PAD + T], F32, name="out_rows%d" % i) for i in range(BATCH * S_BLOCKS)]
         for rows in out_rows:
             nc.vector.memset(rows[:, 0:PAD], 0.0)
 
-        nc.sync.dma_start(out=bias_rows[0:HEADS, :], in_=v_bias.rearrange("o h i k -> (o h i) k"))
         q_raw = [keep.tile([P, S_BLOCKS * K], BF16, name="q_raw%d" % b) for b in range(BATCH)]
         r_raw = [keep.tile([P, ROWS * K], BF16, name="r_raw%d" % i) for i in range(HEADS * T_CHUNKS)]
         for h in HEAD_ORDER:
             for b in range(h, BATCH, HEADS):
                 nc.sync.dma_start(out=q_raw[b][:], in_=queries[b].rearrange("(p e) k -> p (e k)", e=2))
+                if b == HEAD_ORDER[0]:
+                    nc.sync.dma_start(out=bias_rows[0:HEADS, :], in_=v_bias.rearrange("o h i k -> (o h i) k"))
             for c in range(T_CHUNKS):
                 nc.sync.dma_start(
                     out=r_raw[h * T_CHUNKS + c][:],
                     in_=R[h, c * T_CHUNK : (c + 1) * T_CHUNK, :].rearrange("(p j) k -> p (j k)", j=ROWS),
                 )
 
-        warm = psum.tile([P, P], F32, tag="flip")
-        for n in range(4):
-            nc.tensor.matmul(warm[:], lhsT=zeros[:], rhs=zeros[:], start=True, stop=True)
-
-        def keep_warm(loaded):
-            idle = psum.tile([P, T_CHUNK], F32, tag="flip")
-            nc.tensor.matmul(idle[:], lhsT=zeros_bf[:], rhs=loaded[:, 0:T_CHUNK], start=True, stop=True)
-
         bias_sb = keep.tile([P, HEADS * PACK], BF16)
-        bias_t = psum.tile([P, 2 * P], F32, tag="flip")
-        for u in range(2):
-            nc.tensor.transpose(bias_t[:, u * P : (u + 1) * P], bias_rows[:].bitcast(F32)[:, u:WORDS:2], ident[:])
-        nc.vector.tensor_copy(
-            out=bias_sb[:].bitcast(F32).rearrange("p (h u) -> p h u", u=2),
-            in_=bias_t[:].rearrange("p (u s) -> p s u", u=2)[:, 0:HEADS, :],
-        )
+
+        def spread_bias():
+            bias_t = psum.tile([P, 2 * P], F32, tag="flip")
+            for u in range(2):
+                nc.tensor.transpose(bias_t[:, u * P : (u + 1) * P], bias_rows[:].bitcast(F32)[:, u:WORDS:2], ident[:])
+            nc.vector.tensor_copy(
+                out=bias_sb[:].bitcast(F32).rearrange("p (h u) -> p h u", u=2),
+                in_=bias_t[:].rearrange("p (u s) -> p s u", u=2)[:, 0:HEADS, :],
+            )
 
         q_codes = keep.tile([P, BATCH, S], U32, align_bytes=64)
         q_scales = keep.tile([P, BATCH, S], U8, align_bytes=64)
@@ -94,6 +85,8 @@ def tile_relativepositionsdpa_pa_kernel(tc, queries, v_bias, R, out):
             for f in range(4):
                 at = (f // 2) * WORDS + f % 2
                 nc.tensor.transpose(flip[:, f * P : (f + 1) * P], words[:, at : at + WORDS - 1 : 2], ident[:])
+            if b == HEAD_ORDER[0]:
+                spread_bias()
             q_pairs = stage.tile([P, S * PACK], BF16)
             nc.scalar.copy(
                 out=q_pairs[:].bitcast(F32).rearrange("p (n f) -> p n f", f=4),
@@ -172,9 +165,7 @@ def tile_relativepositionsdpa_pa_kernel(tc, queries, v_bias, R, out):
             nc.sync.dma_start(out=view[:, lo - skip : hi - skip], in_=rows[:, PAD - 1 + lo : PAD - 1 + hi])
 
         prepare_queries(1)
-        keep_warm(q_raw[1])
         prepare_queries(3)
-        keep_warm(q_raw[3])
         prepare_table(4)
         prepare_table(5)
         products(1, 0)

@@ -103,7 +103,7 @@ def tile_relativepositionsdpa_pa_kernel(tc, queries, v_bias, R, out):
             )
             nc.vector.quantize_mx(out=q_codes[:, b, :].bitcast(FP8X4), scales=q_scales[:, b, :], in_=q_v[:])
 
-        def prepare_table(i):
+        def turn_table(i):
             words = r_raw[i][:].bitcast(F32)
             grouped = stage.tile([P, T_CHUNK * PACK], BF16, align_bytes=64)
             grouped_words = grouped[:].bitcast(F32).rearrange("p (n g f) -> p n g f", g=2, f=4)
@@ -117,6 +117,9 @@ def tile_relativepositionsdpa_pa_kernel(tc, queries, v_bias, R, out):
                         ident[:],
                     )
                 nc.scalar.copy(out=grouped_words[:, :, g, :], in_=flip[:].rearrange("p (f n) -> p n f", f=4))
+            return grouped
+
+        def quantise_table(i, grouped):
             nc.vector.quantize_mx(out=r_codes[:, i, :].bitcast(FP8X4), scales=r_scales[:, i, :], in_=grouped[:])
 
         def products(b, g):
@@ -164,23 +167,18 @@ def tile_relativepositionsdpa_pa_kernel(tc, queries, v_bias, R, out):
             view = flat[start : start + P * WIDE].rearrange("(p w) -> p w", w=WIDE)
             nc.sync.dma_start(out=view[:, lo - skip : hi - skip], in_=rows[:, PAD - 1 + lo : PAD - 1 + hi])
 
-        prepare_queries(1)
-        prepare_queries(3)
-        prepare_table(4)
-        prepare_table(5)
-        products(1, 0)
-        prepare_table(6)
-        products(3, 0)
-        prepare_table(7)
-        prepare_queries(0)
-        products(1, 1)
-        prepare_table(0)
-        products(3, 1)
-        prepare_table(1)
-        prepare_queries(2)
-        products(0, 0)
-        prepare_table(2)
-        products(2, 0)
-        prepare_table(3)
-        products(0, 1)
-        products(2, 1)
+        with tc.manual_schedule(engines={mybir.EngineType.PE, mybir.EngineType.DVE, mybir.EngineType.Activation}):
+            prepare_queries(1)
+            prepare_queries(3)
+            quantise_table(4, turn_table(4))
+            quantise_table(5, turn_table(5))
+            for chunk, b, g in ((6, 1, 0), (7, 3, 0), (0, 1, 1), (1, 3, 1), (2, 0, 0), (3, 2, 0)):
+                if chunk == 0:
+                    prepare_queries(0)
+                if chunk == 2:
+                    prepare_queries(2)
+                grouped = turn_table(chunk)
+                products(b, g)
+                quantise_table(chunk, grouped)
+            products(0, 1)
+            products(2, 1)

@@ -24,6 +24,7 @@ S_BLOCKS = S // P
 T_CHUNK = 512
 T_CHUNKS = T // T_CHUNK
 ROWS = T_CHUNK // P
+PIECES = {1: (1, 1, 1, 1), 0: (2, 2)}
 PAD = 8
 WIDE = T + 1
 DROP = S
@@ -49,18 +50,24 @@ def tile_relativepositionsdpa_pa_kernel(tc, queries, v_bias, R, out):
         for rows in out_rows:
             nc.vector.memset(rows[:, 0:PAD], 0.0)
 
-        q_raw = [keep.tile([P, S_BLOCKS * K], BF16, name="q_raw%d" % b) for b in range(BATCH)]
-        r_raw = [keep.tile([P, ROWS * K], BF16, name="r_raw%d" % i) for i in range(HEADS * T_CHUNKS)]
+        q_raw = {b: keep.tile([P, S_BLOCKS * K], BF16, name="q_raw%d" % b) for b in range(BATCH)}
+        chunks = {}
         for h in HEAD_ORDER:
             for b in range(h, BATCH, HEADS):
                 nc.sync.dma_start(out=q_raw[b][:], in_=queries[b].rearrange("(p e) k -> p (e k)", e=2))
                 if b == HEAD_ORDER[0]:
                     nc.sync.dma_start(out=bias_rows[0:HEADS, :], in_=v_bias.rearrange("o h i k -> (o h i) k"))
-            for c in range(T_CHUNKS):
+            c = 0
+            for width in PIECES[h]:
+                t0 = c * T_CHUNK
+                raw = keep.tile([P, width * ROWS * K], BF16, name="r_raw_%d_%d" % (h, c))
                 nc.sync.dma_start(
-                    out=r_raw[h * T_CHUNKS + c][:],
-                    in_=R[h, c * T_CHUNK : (c + 1) * T_CHUNK, :].rearrange("(p j) k -> p (j k)", j=ROWS),
+                    out=raw[:],
+                    in_=R[h, t0 : t0 + width * T_CHUNK, :].rearrange("(p j) k -> p (j k)", j=width * ROWS),
                 )
+                for a in range(width):
+                    chunks[h * T_CHUNKS + c + a] = (raw, a, t0, width)
+                c += width
 
         bias_sb = keep.tile([P, HEADS * PACK], BF16)
 
@@ -82,20 +89,26 @@ def tile_relativepositionsdpa_pa_kernel(tc, queries, v_bias, R, out):
             h = b % HEADS
             words = q_raw[b][:].bitcast(F32)
             flip = psum.tile([P, 4 * P], F32, tag="flip")
+            early = h == HEAD_ORDER[0]
             for f in range(4):
                 at = (f // 2) * WORDS + f % 2
-                nc.tensor.transpose(flip[:, f * P : (f + 1) * P], words[:, at : at + WORDS - 1 : 2], ident[:])
+                to = flip[:, f * P : (f + 1) * P] if early else flip[:].rearrange("p (n f) -> p f n", f=4)[:, f, :]
+                nc.tensor.transpose(to, words[:, at : at + WORDS - 1 : 2], ident[:])
             if b == HEAD_ORDER[0]:
                 spread_bias()
-            q_pairs = stage.tile([P, S * PACK], BF16)
-            nc.scalar.copy(
-                out=q_pairs[:].bitcast(F32).rearrange("p (n f) -> p n f", f=4),
-                in_=flip[:].rearrange("p (f n) -> p n f", f=4),
-            )
+            if early:
+                q_pairs = stage.tile([P, S * PACK], BF16)
+                nc.scalar.copy(
+                    out=q_pairs[:].bitcast(F32).rearrange("p (n f) -> p n f", f=4),
+                    in_=flip[:].rearrange("p (f n) -> p n f", f=4),
+                )
+                raw = q_pairs[:]
+            else:
+                raw = flip[:].bitcast(BF16)
             q_v = stage.tile([P, S * PACK], BF16, align_bytes=64)
             nc.vector.scalar_tensor_tensor(
                 out=q_v[:].rearrange("p (s t) -> p s t", t=PACK),
-                in0=q_pairs[:].rearrange("p (s t) -> p s t", t=PACK),
+                in0=raw.rearrange("p (s t) -> p s t", t=PACK),
                 scalar=K**-0.5,
                 in1=bias_sb[:, h * PACK : (h + 1) * PACK].unsqueeze(1).to_broadcast([P, S, PACK]),
                 op0=MULT,
@@ -104,7 +117,8 @@ def tile_relativepositionsdpa_pa_kernel(tc, queries, v_bias, R, out):
             nc.vector.quantize_mx(out=q_codes[:, b, :].bitcast(FP8X4), scales=q_scales[:, b, :], in_=q_v[:])
 
         def turn_table(i):
-            words = r_raw[i][:].bitcast(F32)
+            raw, a = chunks[i][0:2]
+            words = raw[:].bitcast(F32)[:, a * ROWS * WORDS : (a + 1) * ROWS * WORDS]
             grouped = stage.tile([P, T_CHUNK * PACK], BF16, align_bytes=64)
             grouped_words = grouped[:].bitcast(F32).rearrange("p (n g f) -> p n g f", g=2, f=4)
             for g in range(2):
@@ -122,7 +136,7 @@ def tile_relativepositionsdpa_pa_kernel(tc, queries, v_bias, R, out):
         def quantise_table(i, grouped):
             nc.vector.quantize_mx(out=r_codes[:, i, :].bitcast(FP8X4), scales=r_scales[:, i, :], in_=grouped[:])
 
-        def products(b, g):
+        def products(b, g, relieve=False):
             h = b % HEADS
             for j in range(S_BLOCKS):
                 for c in range(g * GROUP, (g + 1) * GROUP):
@@ -137,11 +151,14 @@ def tile_relativepositionsdpa_pa_kernel(tc, queries, v_bias, R, out):
                         start=True,
                         stop=True,
                     )
-                    dst = out_rows[b * S_BLOCKS + j][:, PAD + c * T_CHUNK : PAD + (c + 1) * T_CHUNK]
-                    if c % 2 == 0:
-                        nc.vector.tensor_copy(out=dst, in_=acc[:])
+                    a, t0, width = chunks[i][1:4]
+                    dst = out_rows[b * S_BLOCKS + j][:, PAD + t0 : PAD + t0 + width * T_CHUNK]
+                    dst = dst.rearrange("s (p a f) -> s a p f", a=width, f=ROWS)[:, a, :, :]
+                    src = acc[:].rearrange("s (p f) -> s p f", f=ROWS)
+                    if c % 2 == 0 and not (relieve and j == 1):
+                        nc.vector.tensor_copy(out=dst, in_=src)
                     else:
-                        nc.scalar.copy(out=dst, in_=acc[:])
+                        nc.scalar.copy(out=dst, in_=src)
                 store(b, j, g)
 
         flat = out.rearrange("b s t -> (b s t)")
@@ -178,7 +195,7 @@ def tile_relativepositionsdpa_pa_kernel(tc, queries, v_bias, R, out):
                 if chunk == 2:
                     prepare_queries(2)
                 grouped = turn_table(chunk)
-                products(b, g)
+                products(b, g, relieve=chunk in (0, 2))
                 quantise_table(chunk, grouped)
             products(0, 1)
             products(2, 1)

from contextlib import ExitStack

import concourse.mybir as mybir
from concourse.masks import make_identity

F32 = mybir.dt.float32
BF16 = mybir.dt.bfloat16
U32 = mybir.dt.uint32
U8 = mybir.dt.uint8
FP8X4 = mybir.dt.float8_e4m3fn_x4
MULT = mybir.AluOpType.mult
ADD = mybir.AluOpType.add

P = 128
HEADS = 2
SEQS = 2
BATCH = SEQS * HEADS
S = 256
T = 2048
K = 512
PACK = 4
WORDS = K // 2
S_BLOCKS = S // P
T_CHUNK = 512
T_CHUNKS = T // T_CHUNK
ROWS = T_CHUNK // P
PIECES = {1: (1, 1, 1, 1), 0: (2, 2)}
PAD = 8
WIDE = T + 1
DROP = S
GROUP = 2
HEAD_ORDER = (1, 0)

FLOPS = 2 * BATCH * S * T * K
BYTES = 2 * (BATCH * S * K + HEADS * K + HEADS * T * K) + 4 * BATCH * S * T


def tile_relativepositionsdpa_pa_kernel(tc, queries, v_bias, R, out):
    nc = tc.nc
    with ExitStack() as ctx:
        keep = ctx.enter_context(tc.tile_pool(name="keep", bufs=1))
        stage = ctx.enter_context(tc.tile_pool(name="stage", bufs=3))
        psum = ctx.enter_context(tc.psum_pool(name="psum", bufs=4))

        ident = keep.tile([P, P], F32)
        make_identity(nc, ident[:])
        bias_rows = keep.tile([P, K], BF16)
        nc.vector.memset(bias_rows[:].bitcast(F32), 0.0)
        out_rows = [keep.tile([P, PAD + T], F32, name="out_rows%d" % i) for i in range(BATCH * S_BLOCKS)]
        for rows in out_rows:
            nc.vector.memset(rows[:, 0:PAD], 0.0)

        q_raw = {b: keep.tile([P, S_BLOCKS * K], BF16, name="q_raw%d" % b) for b in range(BATCH)}
        chunks = {}
        for h in HEAD_ORDER:
            for b in range(h, BATCH, HEADS):
                nc.sync.dma_start(out=q_raw[b][:], in_=queries[b].rearrange("(p e) k -> p (e k)", e=2))
                if b == HEAD_ORDER[0]:
                    nc.sync.dma_start(out=bias_rows[0:HEADS, :], in_=v_bias.rearrange("o h i k -> (o h i) k"))
            c = 0
            for width in PIECES[h]:
                t0 = c * T_CHUNK
                raw = keep.tile([P, width * ROWS * K], BF16, name="r_raw_%d_%d" % (h, c))
                nc.sync.dma_start(
                    out=raw[:],
                    in_=R[h, t0 : t0 + width * T_CHUNK, :].rearrange("(p j) k -> p (j k)", j=width * ROWS),
                )
                for a in range(width):
                    chunks[h * T_CHUNKS + c + a] = (raw, a, t0, width)
                c += width

        bias_sb = keep.tile([P, HEADS * PACK], BF16)

        def spread_bias():
            bias_t = psum.tile([P, 2 * P], F32, tag="flip")
            for u in range(2):
                nc.tensor.transpose(bias_t[:, u * P : (u + 1) * P], bias_rows[:].bitcast(F32)[:, u:WORDS:2], ident[:])
            nc.vector.tensor_copy(
                out=bias_sb[:].bitcast(F32).rearrange("p (h u) -> p h u", u=2),
                in_=bias_t[:].rearrange("p (u s) -> p s u", u=2)[:, 0:HEADS, :],
            )

        q_codes = keep.tile([P, BATCH, S], U32, align_bytes=64)
        q_scales = keep.tile([P, BATCH, S], U8, align_bytes=64)
        r_codes = keep.tile([P, HEADS * T_CHUNKS, T_CHUNK], U32, align_bytes=64)
        r_scales = keep.tile([P, HEADS * T_CHUNKS, T_CHUNK], U8, align_bytes=64)

        def prepare_queries(b):
            h = b % HEADS
            words = q_raw[b][:].bitcast(F32)
            flip = psum.tile([P, 4 * P], F32, tag="flip")
            early = h == HEAD_ORDER[0]
            for f in range(4):
                at = (f // 2) * WORDS + f % 2
                to = flip[:, f * P : (f + 1) * P] if early else flip[:].rearrange("p (n f) -> p f n", f=4)[:, f, :]
                nc.tensor.transpose(to, words[:, at : at + WORDS - 1 : 2], ident[:])
            if b == HEAD_ORDER[0]:
                spread_bias()
            if early:
                q_pairs = stage.tile([P, S * PACK], BF16)
                nc.scalar.copy(
                    out=q_pairs[:].bitcast(F32).rearrange("p (n f) -> p n f", f=4),
                    in_=flip[:].rearrange("p (f n) -> p n f", f=4),
                )
                raw = q_pairs[:]
            else:
                raw = flip[:].bitcast(BF16)
            q_v = stage.tile([P, S * PACK], BF16, align_bytes=64)
            nc.vector.scalar_tensor_tensor(
                out=q_v[:].rearrange("p (s t) -> p s t", t=PACK),
                in0=raw.rearrange("p (s t) -> p s t", t=PACK),
                scalar=K**-0.5,
                in1=bias_sb[:, h * PACK : (h + 1) * PACK].unsqueeze(1).to_broadcast([P, S, PACK]),
                op0=MULT,
                op1=ADD,
            )
            nc.vector.quantize_mx(out=q_codes[:, b, :].bitcast(FP8X4), scales=q_scales[:, b, :], in_=q_v[:])

        def turn_table(i):
            raw, a = chunks[i][0:2]
            words = raw[:].bitcast(F32)[:, a * ROWS * WORDS : (a + 1) * ROWS * WORDS]
            grouped = stage.tile([P, T_CHUNK * PACK], BF16, align_bytes=64)
            grouped_words = grouped[:].bitcast(F32).rearrange("p (n g f) -> p n g f", g=2, f=4)
            for g in range(2):
                flip = psum.tile([P, 4 * P], F32, tag="flip")
                for f in range(4):
                    j, u = 2 * g + f // 2, f % 2
                    nc.tensor.transpose(
                        flip[:, f * P : (f + 1) * P],
                        words[:, j * WORDS + u : (j + 1) * WORDS : 2],
                        ident[:],
                    )
                nc.scalar.copy(out=grouped_words[:, :, g, :], in_=flip[:].rearrange("p (f n) -> p n f", f=4))
            return grouped

        def quantise_table(i, grouped):
            nc.vector.quantize_mx(out=r_codes[:, i, :].bitcast(FP8X4), scales=r_scales[:, i, :], in_=grouped[:])

        def products(b, g, relieve=False):
            h = b % HEADS
            for j in range(S_BLOCKS):
                for c in range(g * GROUP, (g + 1) * GROUP):
                    i = h * T_CHUNKS + c
                    acc = psum.tile([P, T_CHUNK], F32, tag="acc")
                    nc.tensor.matmul_mx(
                        out=acc[:],
                        lhsT=q_codes[:, b, j * P : (j + 1) * P].bitcast(FP8X4),
                        lhsT_scale=q_scales[:, b, j * P : (j + 1) * P],
                        rhs=r_codes[:, i, :].bitcast(FP8X4),
                        rhs_scale=r_scales[:, i, :],
                        start=True,
                        stop=True,
                    )
                    a, t0, width = chunks[i][1:4]
                    dst = out_rows[b * S_BLOCKS + j][:, PAD + t0 : PAD + t0 + width * T_CHUNK]
                    dst = dst.rearrange("s (p a f) -> s a p f", a=width, f=ROWS)[:, a, :, :]
                    src = acc[:].rearrange("s (p f) -> s p f", f=ROWS)
                    if c % 2 == 0 and not (relieve and j == 1):
                        nc.vector.tensor_copy(out=dst, in_=src)
                    else:
                        nc.scalar.copy(out=dst, in_=src)
                store(b, j, g)

        flat = out.rearrange("b s t -> (b s t)")
        held = []

        def store(b, j, g):
            for late in held:
                late()
            held.clear()
            rows = out_rows[b * S_BLOCKS + j]
            lo = 1 + g * GROUP * T_CHUNK if g > 0 else 0
            hi = 1 + (g + 1) * GROUP * T_CHUNK
            if b % HEADS == 0 and j == 0:
                start, skip = b * S * T, DROP
                if g == 0:
                    later = flat[start + WIDE - DROP : start + P * WIDE - DROP].rearrange("(p w) -> p w", w=WIDE)
                    front = slice(PAD - 1, PAD - 1 + DROP)
                    nc.sync.dma_start(out=later[P // 2 - 1 : P - 1, 0:DROP], in_=rows[P // 2 : P, front])
                    held.append(lambda: nc.sync.dma_start(out=later[0 : P // 2, 0:DROP], in_=rows[1 : P // 2 + 1, front]))
                    lo = DROP
            else:
                start, skip = b * S * T + j * P * WIDE - DROP, 0
            view = flat[start : start + P * WIDE].rearrange("(p w) -> p w", w=WIDE)
            nc.sync.dma_start(out=view[:, lo - skip : hi - skip], in_=rows[:, PAD - 1 + lo : PAD - 1 + hi])

        with tc.manual_schedule(engines={mybir.EngineType.PE, mybir.EngineType.DVE, mybir.EngineType.Activation}):
            prepare_queries(1)
            prepare_queries(3)
            quantise_table(4, turn_table(4))
            quantise_table(5, turn_table(5))
            for chunk, b, g in ((6, 1, 0), (7, 3, 0), (0, 1, 1), (1, 3, 1), (2, 0, 0), (3, 2, 0)):
                if chunk == 0:
                    prepare_queries(0)
                if chunk == 2:
                    prepare_queries(2)
                grouped = turn_table(chunk)
                products(b, g, relieve=chunk in (0, 2))
                quantise_table(chunk, grouped)
            products(0, 1)
            products(2, 1)
